import numpy as np
import ml_dtypes

BF16 = ml_dtypes.bfloat16


def bf(x):
    return np.asarray(x, np.float32).astype(BF16)


def f32(x):
    return np.asarray(x, np.float32)


def f64(x):
    return np.asarray(x).astype(np.float64)


def striped(idx):
    return np.tile(idx.reshape(-1, 16).T, (8, 1))


C, S, N = 512, 2048, 1024


def hadamard(n):
    h = np.ones((1, 1))
    while h.shape[0] < n:
        h = np.block([[h, h], [h, -h]])
    return h / np.sqrt(n)


def setup_inputs():
    base = f32(np.random.standard_normal((C, S)))
    value = f32(np.random.standard_normal((C, N)))
    signs = np.sign(np.random.standard_normal((N, 1)))
    weight = f32(signs * hadamard(N))
    return {"base": base, "value": value, "weight": weight, "offs": striped(np.random.permutation(S)[:N])}


def reference(base, value, weight, offs):
    idx = offs[:16].T.reshape(-1)
    out = f64(base).copy()
    out[:, idx] = f64(value) @ f64(weight) + f64(value)
    return out

@@ -1,0 +1,79 @@
+import concourse.mybir as mybir
+from concourse.masks import make_identity
+
+F32 = mybir.dt.float32
+BF16 = mybir.dt.bfloat16
+U16 = mybir.dt.uint16
+ADD = mybir.AluOpType.add
+COPY = mybir.ActivationFunctionType.Copy
+
+P = 128
+TOKENS = 512
+HIDDEN = 1024
+WIDE = 2048
+BANK = 512
+
+BLOCKS = TOKENS // P
+K_TILES = HIDDEN // P
+HALVES = HIDDEN // BANK
+
+FLOPS = 2 * TOKENS * HIDDEN * HIDDEN
+
+
+def tile_hadamardtransform_kernel(tc, base, value, weight, offs, out):
+    nc = tc.nc
+    with (
+        tc.tile_pool(name="held", bufs=1) as held,
+        tc.psum_pool(name="flip_psum", bufs=2) as flip_psum,
+        tc.psum_pool(name="acc_psum", bufs=2) as acc_psum,
+    ):
+        offsets = held.tile([P, HIDDEN // 16], U16, name="offsets")
+        nc.sync.dma_start(offsets[:], offs)
+
+        identity = held.tile([P, P], F32, name="identity")
+        make_identity(nc, identity[:])
+
+        tokens = [held.tile([P, HIDDEN], F32, name=f"tokens{b}") for b in range(BLOCKS)]
+        windows = [held.tile([P, WIDE], F32, name=f"window{b}") for b in range(BLOCKS)]
+        weight_f32 = [held.tile([P, HIDDEN], F32, name=f"weight_f32_{k}") for k in range(K_TILES)]
+
+        nc.sync.dma_start(tokens[0][:], value[0:P, :])
+        for k in range(K_TILES):
+            nc.sync.dma_start(weight_f32[k][:], weight[k * P : (k + 1) * P, :])
+        nc.sync.dma_start(windows[0][:], base[0:P, :])
+        for b in range(1, BLOCKS):
+            nc.sync.dma_start(tokens[b][:], value[b * P : (b + 1) * P, :])
+            nc.sync.dma_start(windows[b][:], base[b * P : (b + 1) * P, :])
+
+        weight_bf = [held.tile([P, HIDDEN], BF16, name=f"weight_bf{k}") for k in range(K_TILES)]
+        for k in range(K_TILES):
+            nc.vector.tensor_copy(weight_bf[k][:], weight_f32[k][:])
+
+        for b in range(BLOCKS):
+            tokens_t = held.tile([P, HIDDEN], BF16, name=f"tokens_t{b}")
+            for h in range(HALVES):
+                flipped = flip_psum.tile([P, BANK], F32, name="flipped")
+                for q in range(BANK // P):
+                    k = h * (BANK // P) + q
+                    nc.tensor.transpose(
+                        flipped[:, q * P : (q + 1) * P], tokens[b][:, k * P : (k + 1) * P], identity[:]
+                    )
+                nc.scalar.activation(tokens_t[:, h * BANK : (h + 1) * BANK], flipped[:], COPY)
+
+            acc = [acc_psum.tile([P, BANK], F32, name=f"acc{h}") for h in range(HALVES)]
+            for k in range(K_TILES):
+                for h in range(HALVES):
+                    nc.tensor.matmul(
+                        acc[h][:],
+                        tokens_t[:, k * P : (k + 1) * P],
+                        weight_bf[k][:, h * BANK : (h + 1) * BANK],
+                        start=(k == 0),
+                        stop=(k == K_TILES - 1),
+                    )
+
+            rotated = held.tile([P, HIDDEN], F32, name=f"rotated{b}")
+            for h in range(HALVES):
+                nc.scalar.activation(rotated[:, h * BANK : (h + 1) * BANK], acc[h][:], COPY)
+
+            nc.vector.tensor_tensor(windows[b][:].indirect(offsets[:]), rotated[:], tokens[b][:], ADD)
+            nc.sync.dma_start(out[b * P : (b + 1) * P, :], windows[b][:])

@@ -35,19 +35,34 @@ def tile_hadamardtransform_kernel(tc, base, value, weight, offs, out):
 
         tokens = [held.tile([P, HIDDEN], F32, name=f"tokens{b}") for b in range(BLOCKS)]
         windows = [held.tile([P, WIDE], F32, name=f"window{b}") for b in range(BLOCKS)]
-        weight_f32 = [held.tile([P, HIDDEN], F32, name=f"weight_f32_{k}") for k in range(K_TILES)]
+        weight_f32 = [
+            [held.tile([P, BANK], F32, name=f"weight_f32_{h}_{k}") for k in range(K_TILES)] for h in range(HALVES)
+        ]
 
-        nc.sync.dma_start(tokens[0][:], value[0:P, :])
-        for k in range(K_TILES):
-            nc.sync.dma_start(weight_f32[k][:], weight[k * P : (k + 1) * P, :])
-        nc.sync.dma_start(windows[0][:], base[0:P, :])
-        for b in range(1, BLOCKS):
+        def load_tokens(b):
             nc.sync.dma_start(tokens[b][:], value[b * P : (b + 1) * P, :])
+
+        def load_window(b):
             nc.sync.dma_start(windows[b][:], base[b * P : (b + 1) * P, :])
 
-        weight_bf = [held.tile([P, HIDDEN], BF16, name=f"weight_bf{k}") for k in range(K_TILES)]
-        for k in range(K_TILES):
-            nc.vector.tensor_copy(weight_bf[k][:], weight_f32[k][:])
+        load_tokens(0)
+        load_tokens(1)
+        for h in range(HALVES):
+            for k in range(K_TILES):
+                nc.sync.dma_start(weight_f32[h][k][:], weight[k * P : (k + 1) * P, h * BANK : (h + 1) * BANK])
+        load_window(0)
+        load_tokens(2)
+        load_tokens(3)
+        load_window(1)
+        load_window(2)
+        load_window(3)
+
+        weight_bf = [
+            [held.tile([P, BANK], BF16, name=f"weight_bf{h}_{k}") for k in range(K_TILES)] for h in range(HALVES)
+        ]
+        for h in range(HALVES):
+            for k in range(K_TILES):
+                nc.vector.tensor_copy(weight_bf[h][k][:], weight_f32[h][k][:])
 
         for b in range(BLOCKS):
             tokens_t = held.tile([P, HIDDEN], BF16, name=f"tokens_t{b}")
@@ -61,12 +76,12 @@ def tile_hadamardtransform_kernel(tc, base, value, weight, offs, out):
                 nc.scalar.activation(tokens_t[:, h * BANK : (h + 1) * BANK], flipped[:], COPY)
 
             acc = [acc_psum.tile([P, BANK], F32, name=f"acc{h}") for h in range(HALVES)]
-            for k in range(K_TILES):
-                for h in range(HALVES):
+            for h in range(HALVES):
+                for k in range(K_TILES):
                     nc.tensor.matmul(
                         acc[h][:],
                         tokens_t[:, k * P : (k + 1) * P],
-                        weight_bf[k][:, h * BANK : (h + 1) * BANK],
+                        weight_bf[h][k][:],
                         start=(k == 0),
                         stop=(k == K_TILES - 1),
                     )

@@ -46,10 +46,10 @@ def tile_hadamardtransform_kernel(tc, base, value, weight, offs, out):
             nc.sync.dma_start(windows[b][:], base[b * P : (b + 1) * P, :])
 
         load_tokens(0)
-        load_tokens(1)
         for h in range(HALVES):
             for k in range(K_TILES):
                 nc.sync.dma_start(weight_f32[h][k][:], weight[k * P : (k + 1) * P, h * BANK : (h + 1) * BANK])
+        load_tokens(1)
         load_window(0)
         load_tokens(2)
         load_tokens(3)

@@ -35,9 +35,7 @@ def tile_hadamardtransform_kernel(tc, base, value, weight, offs, out):
 
         tokens = [held.tile([P, HIDDEN], F32, name=f"tokens{b}") for b in range(BLOCKS)]
         windows = [held.tile([P, WIDE], F32, name=f"window{b}") for b in range(BLOCKS)]
-        weight_f32 = [
-            [held.tile([P, BANK], F32, name=f"weight_f32_{h}_{k}") for k in range(K_TILES)] for h in range(HALVES)
-        ]
+        weight_f32 = [held.tile([P, HIDDEN], F32, name=f"weight_f32_{k}") for k in range(K_TILES)]
 
         def load_tokens(b):
             nc.sync.dma_start(tokens[b][:], value[b * P : (b + 1) * P, :])
@@ -46,9 +44,8 @@ def tile_hadamardtransform_kernel(tc, base, value, weight, offs, out):
             nc.sync.dma_start(windows[b][:], base[b * P : (b + 1) * P, :])
 
         load_tokens(0)
-        for h in range(HALVES):
-            for k in range(K_TILES):
-                nc.sync.dma_start(weight_f32[h][k][:], weight[k * P : (k + 1) * P, h * BANK : (h + 1) * BANK])
+        for k in range(K_TILES):
+            nc.sync.dma_start(weight_f32[k][:], weight[k * P : (k + 1) * P, :])
         load_tokens(1)
         load_window(0)
         load_tokens(2)
@@ -57,12 +54,9 @@ def tile_hadamardtransform_kernel(tc, base, value, weight, offs, out):
         load_window(2)
         load_window(3)
 
-        weight_bf = [
-            [held.tile([P, BANK], BF16, name=f"weight_bf{h}_{k}") for k in range(K_TILES)] for h in range(HALVES)
-        ]
-        for h in range(HALVES):
-            for k in range(K_TILES):
-                nc.vector.tensor_copy(weight_bf[h][k][:], weight_f32[h][k][:])
+        weight_bf = [held.tile([P, HIDDEN], BF16, name=f"weight_bf{k}") for k in range(K_TILES)]
+        for k in range(K_TILES):
+            nc.vector.tensor_copy(weight_bf[k][:], weight_f32[k][:])
 
         for b in range(BLOCKS):
             tokens_t = held.tile([P, HIDDEN], BF16, name=f"tokens_t{b}")
@@ -76,12 +70,12 @@ def tile_hadamardtransform_kernel(tc, base, value, weight, offs, out):
                 nc.scalar.activation(tokens_t[:, h * BANK : (h + 1) * BANK], flipped[:], COPY)
 
             acc = [acc_psum.tile([P, BANK], F32, name=f"acc{h}") for h in range(HALVES)]
-            for h in range(HALVES):
-                for k in range(K_TILES):
+            for k in range(K_TILES):
+                for h in range(HALVES):
                     nc.tensor.matmul(
                         acc[h][:],
                         tokens_t[:, k * P : (k + 1) * P],
-                        weight_bf[h][k][:],
+                        weight_bf[k][:, h * BANK : (h + 1) * BANK],
                         start=(k == 0),
                         stop=(k == K_TILES - 1),
                     )

@@ -16,6 +16,8 @@ BANK = 512
 BLOCKS = TOKENS // P
 K_TILES = HIDDEN // P
 HALVES = HIDDEN // BANK
+PAIR = 2
+PAIRS = K_TILES // PAIR
 
 FLOPS = 2 * TOKENS * HIDDEN * HIDDEN
 
@@ -24,7 +26,7 @@ def tile_hadamardtransform_kernel(tc, base, value, weight, offs, out):
     nc = tc.nc
     with (
         tc.tile_pool(name="held", bufs=1) as held,
-        tc.psum_pool(name="flip_psum", bufs=2) as flip_psum,
+        tc.psum_pool(name="flip_psum", bufs=4) as flip_psum,
         tc.psum_pool(name="acc_psum", bufs=2) as acc_psum,
     ):
         offsets = held.tile([P, HIDDEN // 16], U16, name="offsets")
@@ -37,8 +39,9 @@ def tile_hadamardtransform_kernel(tc, base, value, weight, offs, out):
         windows = [held.tile([P, WIDE], F32, name=f"window{b}") for b in range(BLOCKS)]
         weight_f32 = [held.tile([P, HIDDEN], F32, name=f"weight_f32_{k}") for k in range(K_TILES)]
 
-        def load_tokens(b):
-            nc.sync.dma_start(tokens[b][:], value[b * P : (b + 1) * P, :])
+        def load_tokens(b, first_pair=0, last_pair=PAIRS):
+            cols = slice(first_pair * PAIR * P, last_pair * PAIR * P)
+            nc.sync.dma_start(tokens[b][:, cols], value[b * P : (b + 1) * P, cols])
 
         def load_window(b):
             nc.sync.dma_start(windows[b][:], base[b * P : (b + 1) * P, :])
@@ -46,39 +49,43 @@ def tile_hadamardtransform_kernel(tc, base, value, weight, offs, out):
         load_tokens(0)
         for k in range(K_TILES):
             nc.sync.dma_start(weight_f32[k][:], weight[k * P : (k + 1) * P, :])
-        load_tokens(1)
+        load_tokens(1, 0, 1)
         load_window(0)
+        load_tokens(1, 1, PAIRS)
         load_tokens(2)
-        load_tokens(3)
         load_window(1)
+        load_tokens(3)
         load_window(2)
         load_window(3)
 
         weight_bf = [held.tile([P, HIDDEN], BF16, name=f"weight_bf{k}") for k in range(K_TILES)]
         for k in range(K_TILES):
-            nc.vector.tensor_copy(weight_bf[k][:], weight_f32[k][:])
+            for h in range(HALVES):
+                cols = slice(h * BANK, (h + 1) * BANK)
+                nc.vector.tensor_copy(weight_bf[k][:, cols], weight_f32[k][:, cols])
 
         for b in range(BLOCKS):
             tokens_t = held.tile([P, HIDDEN], BF16, name=f"tokens_t{b}")
-            for h in range(HALVES):
-                flipped = flip_psum.tile([P, BANK], F32, name="flipped")
-                for q in range(BANK // P):
-                    k = h * (BANK // P) + q
+            for g in range(PAIRS):
+                flipped = flip_psum.tile([P, PAIR * P], F32, name="flipped")
+                for q in range(PAIR):
+                    k = g * PAIR + q
                     nc.tensor.transpose(
                         flipped[:, q * P : (q + 1) * P], tokens[b][:, k * P : (k + 1) * P], identity[:]
                     )
-                nc.scalar.activation(tokens_t[:, h * BANK : (h + 1) * BANK], flipped[:], COPY)
+                nc.scalar.activation(tokens_t[:, g * PAIR * P : (g + 1) * PAIR * P], flipped[:], COPY)
 
             acc = [acc_psum.tile([P, BANK], F32, name=f"acc{h}") for h in range(HALVES)]
-            for k in range(K_TILES):
+            for g in range(PAIRS):
                 for h in range(HALVES):
-                    nc.tensor.matmul(
-                        acc[h][:],
-                        tokens_t[:, k * P : (k + 1) * P],
-                        weight_bf[k][:, h * BANK : (h + 1) * BANK],
-                        start=(k == 0),
-                        stop=(k == K_TILES - 1),
-                    )
+                    for k in range(g * PAIR, (g + 1) * PAIR):
+                        nc.tensor.matmul(
+                            acc[h][:],
+                            tokens_t[:, k * P : (k + 1) * P],
+                            weight_bf[k][:, h * BANK : (h + 1) * BANK],
+                            start=(k == 0),
+                            stop=(k == K_TILES - 1),
+                        )
 
             rotated = held.tile([P, HIDDEN], F32, name=f"rotated{b}")
             for h in range(HALVES):

@@ -89,7 +89,10 @@ def tile_hadamardtransform_kernel(tc, base, value, weight, offs, out):
 
             rotated = held.tile([P, HIDDEN], F32, name=f"rotated{b}")
             for h in range(HALVES):
-                nc.scalar.activation(rotated[:, h * BANK : (h + 1) * BANK], acc[h][:], COPY)
+                if b == 0 and h == 0:
+                    nc.vector.tensor_copy(rotated[:, h * BANK : (h + 1) * BANK], acc[h][:])
+                else:
+                    nc.scalar.activation(rotated[:, h * BANK : (h + 1) * BANK], acc[h][:], COPY)
 
             nc.vector.tensor_tensor(windows[b][:].indirect(offsets[:]), rotated[:], tokens[b][:], ADD)
             nc.sync.dma_start(out[b * P : (b + 1) * P, :], windows[b][:])

@@ -16,8 +16,8 @@ BANK = 512
 BLOCKS = TOKENS // P
 K_TILES = HIDDEN // P
 HALVES = HIDDEN // BANK
-PAIR = 2
-PAIRS = K_TILES // PAIR
+
+STEPS = [range(0, 1), range(1, 2)] + [range(k, k + 2) for k in range(2, K_TILES, 2)]
 
 FLOPS = 2 * TOKENS * HIDDEN * HIDDEN
 
@@ -39,8 +39,8 @@ def tile_hadamardtransform_kernel(tc, base, value, weight, offs, out):
         windows = [held.tile([P, WIDE], F32, name=f"window{b}") for b in range(BLOCKS)]
         weight_f32 = [held.tile([P, HIDDEN], F32, name=f"weight_f32_{k}") for k in range(K_TILES)]
 
-        def load_tokens(b, first_pair=0, last_pair=PAIRS):
-            cols = slice(first_pair * PAIR * P, last_pair * PAIR * P)
+        def load_tokens(b, first=0, last=K_TILES):
+            cols = slice(first * P, last * P)
             nc.sync.dma_start(tokens[b][:, cols], value[b * P : (b + 1) * P, cols])
 
         def load_window(b):
@@ -49,9 +49,11 @@ def tile_hadamardtransform_kernel(tc, base, value, weight, offs, out):
         load_tokens(0)
         for k in range(K_TILES):
             nc.sync.dma_start(weight_f32[k][:], weight[k * P : (k + 1) * P, :])
-        load_tokens(1, 0, 1)
         load_window(0)
-        load_tokens(1, 1, PAIRS)
+        load_tokens(1, 0, 1)
+        load_tokens(1, 1, 2)
+        load_tokens(1, 2, 4)
+        load_tokens(1, 4, K_TILES)
         load_tokens(2)
         load_window(1)
         load_tokens(3)
@@ -66,26 +68,37 @@ def tile_hadamardtransform_kernel(tc, base, value, weight, offs, out):
 
         for b in range(BLOCKS):
             tokens_t = held.tile([P, HIDDEN], BF16, name=f"tokens_t{b}")
-            for g in range(PAIRS):
-                flipped = flip_psum.tile([P, PAIR * P], F32, name="flipped")
-                for q in range(PAIR):
-                    k = g * PAIR + q
+
+            def flip(step):
+                flipped = flip_psum.tile([P, len(step) * P], F32, name="flipped")
+                for q, k in enumerate(step):
                     nc.tensor.transpose(
                         flipped[:, q * P : (q + 1) * P], tokens[b][:, k * P : (k + 1) * P], identity[:]
                     )
-                nc.scalar.activation(tokens_t[:, g * PAIR * P : (g + 1) * PAIR * P], flipped[:], COPY)
+                nc.scalar.activation(tokens_t[:, step[0] * P : (step[-1] + 1) * P], flipped[:], COPY)
 
             acc = [acc_psum.tile([P, BANK], F32, name=f"acc{h}") for h in range(HALVES)]
-            for g in range(PAIRS):
-                for h in range(HALVES):
-                    for k in range(g * PAIR, (g + 1) * PAIR):
-                        nc.tensor.matmul(
-                            acc[h][:],
-                            tokens_t[:, k * P : (k + 1) * P],
-                            weight_bf[k][:, h * BANK : (h + 1) * BANK],
-                            start=(k == 0),
-                            stop=(k == K_TILES - 1),
-                        )
+
+            def multiply(k, h):
+                nc.tensor.matmul(
+                    acc[h][:],
+                    tokens_t[:, k * P : (k + 1) * P],
+                    weight_bf[k][:, h * BANK : (h + 1) * BANK],
+                    start=(k == 0),
+                    stop=(k == K_TILES - 1),
+                )
+
+            last_steps = 1 if b == 0 else 2
+            for i, step in enumerate(STEPS):
+                flip(step)
+                if 0 < i <= len(STEPS) - last_steps:
+                    for h in range(HALVES):
+                        for k in STEPS[i - 1]:
+                            multiply(k, h)
+            for h in range(HALVES):
+                for step in STEPS[-last_steps:]:
+                    for k in step:
+                        multiply(k, h)
 
             rotated = held.tile([P, HIDDEN], F32, name=f"rotated{b}")
             for h in range(HALVES):

@@ -17,6 +17,8 @@ BLOCKS = TOKENS // P
 K_TILES = HIDDEN // P
 HALVES = HIDDEN // BANK
 
+PIECES = (slice(0, BANK), slice(BANK, BANK + BANK // 2), slice(BANK + BANK // 2, HIDDEN))
+
 STEPS = [range(0, 1), range(1, 2)] + [range(k, k + 2) for k in range(2, K_TILES, 2)]
 
 FLOPS = 2 * TOKENS * HIDDEN * HIDDEN
@@ -26,7 +28,7 @@ def tile_hadamardtransform_kernel(tc, base, value, weight, offs, out):
     nc = tc.nc
     with (
         tc.tile_pool(name="held", bufs=1) as held,
-        tc.psum_pool(name="flip_psum", bufs=4) as flip_psum,
+        tc.psum_pool(name="flip_psum", bufs=2) as flip_psum,
         tc.psum_pool(name="acc_psum", bufs=2) as acc_psum,
     ):
         offsets = held.tile([P, HIDDEN // 16], U16, name="offsets")
@@ -77,13 +79,15 @@ def tile_hadamardtransform_kernel(tc, base, value, weight, offs, out):
                     )
                 nc.scalar.activation(tokens_t[:, step[0] * P : (step[-1] + 1) * P], flipped[:], COPY)
 
-            acc = [acc_psum.tile([P, BANK], F32, name=f"acc{h}") for h in range(HALVES)]
+            acc = [
+                acc_psum.tile([P, cols.stop - cols.start], F32, name=f"acc{h}") for h, cols in enumerate(PIECES)
+            ]
 
             def multiply(k, h):
                 nc.tensor.matmul(
                     acc[h][:],
                     tokens_t[:, k * P : (k + 1) * P],
-                    weight_bf[k][:, h * BANK : (h + 1) * BANK],
+                    weight_bf[k][:, PIECES[h]],
                     start=(k == 0),
                     stop=(k == K_TILES - 1),
                 )
@@ -92,20 +96,20 @@ def tile_hadamardtransform_kernel(tc, base, value, weight, offs, out):
             for i, step in enumerate(STEPS):
                 flip(step)
                 if 0 < i <= len(STEPS) - last_steps:
-                    for h in range(HALVES):
+                    for h in range(len(PIECES)):
                         for k in STEPS[i - 1]:
                             multiply(k, h)
-            for h in range(HALVES):
+            for h in range(len(PIECES)):
                 for step in STEPS[-last_steps:]:
                     for k in step:
                         multiply(k, h)
 
             rotated = held.tile([P, HIDDEN], F32, name=f"rotated{b}")
-            for h in range(HALVES):
+            for h, cols in enumerate(PIECES):
                 if b == 0 and h == 0:
-                    nc.vector.tensor_copy(rotated[:, h * BANK : (h + 1) * BANK], acc[h][:])
+                    nc.vector.tensor_copy(rotated[:, cols], acc[h][:])
                 else:
-                    nc.scalar.activation(rotated[:, h * BANK : (h + 1) * BANK], acc[h][:], COPY)
+                    nc.scalar.activation(rotated[:, cols], acc[h][:], COPY)
 
             nc.vector.tensor_tensor(windows[b][:].indirect(offsets[:]), rotated[:], tokens[b][:], ADD)
             nc.sync.dma_start(out[b * P : (b + 1) * P, :], windows[b][:])

@@ -32,8 +32,6 @@ def tile_hadamardtransform_kernel(tc, base, value, weight, offs, out):
         tc.psum_pool(name="acc_psum", bufs=2) as acc_psum,
     ):
         offsets = held.tile([P, HIDDEN // 16], U16, name="offsets")
-        nc.sync.dma_start(offsets[:], offs)
-
         identity = held.tile([P, P], F32, name="identity")
         make_identity(nc, identity[:])
 
@@ -51,6 +49,7 @@ def tile_hadamardtransform_kernel(tc, base, value, weight, offs, out):
         load_tokens(0)
         for k in range(K_TILES):
             nc.sync.dma_start(weight_f32[k][:], weight[k * P : (k + 1) * P, :])
+        nc.sync.dma_start(offsets[:], offs)
         load_window(0)
         load_tokens(1, 0, 1)
         load_tokens(1, 1, 2)

import concourse.mybir as mybir
from concourse.masks import make_identity

F32 = mybir.dt.float32
BF16 = mybir.dt.bfloat16
U16 = mybir.dt.uint16
ADD = mybir.AluOpType.add
COPY = mybir.ActivationFunctionType.Copy

P = 128
TOKENS = 512
HIDDEN = 1024
WIDE = 2048
BANK = 512

BLOCKS = TOKENS // P
K_TILES = HIDDEN // P
HALVES = HIDDEN // BANK

PIECES = (slice(0, BANK), slice(BANK, BANK + BANK // 2), slice(BANK + BANK // 2, HIDDEN))

STEPS = [range(0, 1), range(1, 2)] + [range(k, k + 2) for k in range(2, K_TILES, 2)]

FLOPS = 2 * TOKENS * HIDDEN * HIDDEN


def tile_hadamardtransform_kernel(tc, base, value, weight, offs, out):
    nc = tc.nc
    with (
        tc.tile_pool(name="held", bufs=1) as held,
        tc.psum_pool(name="flip_psum", bufs=2) as flip_psum,
        tc.psum_pool(name="acc_psum", bufs=2) as acc_psum,
    ):
        offsets = held.tile([P, HIDDEN // 16], U16, name="offsets")
        identity = held.tile([P, P], F32, name="identity")
        make_identity(nc, identity[:])

        tokens = [held.tile([P, HIDDEN], F32, name=f"tokens{b}") for b in range(BLOCKS)]
        windows = [held.tile([P, WIDE], F32, name=f"window{b}") for b in range(BLOCKS)]
        weight_f32 = [held.tile([P, HIDDEN], F32, name=f"weight_f32_{k}") for k in range(K_TILES)]

        def load_tokens(b, first=0, last=K_TILES):
            cols = slice(first * P, last * P)
            nc.sync.dma_start(tokens[b][:, cols], value[b * P : (b + 1) * P, cols])

        def load_window(b):
            nc.sync.dma_start(windows[b][:], base[b * P : (b + 1) * P, :])

        load_tokens(0)
        for k in range(K_TILES):
            nc.sync.dma_start(weight_f32[k][:], weight[k * P : (k + 1) * P, :])
        nc.sync.dma_start(offsets[:], offs)
        load_window(0)
        load_tokens(1, 0, 1)
        load_tokens(1, 1, 2)
        load_tokens(1, 2, 4)
        load_tokens(1, 4, K_TILES)
        load_tokens(2)
        load_window(1)
        load_tokens(3)
        load_window(2)
        load_window(3)

        weight_bf = [held.tile([P, HIDDEN], BF16, name=f"weight_bf{k}") for k in range(K_TILES)]
        for k in range(K_TILES):
            for h in range(HALVES):
                cols = slice(h * BANK, (h + 1) * BANK)
                nc.vector.tensor_copy(weight_bf[k][:, cols], weight_f32[k][:, cols])

        for b in range(BLOCKS):
            tokens_t = held.tile([P, HIDDEN], BF16, name=f"tokens_t{b}")

            def flip(step):
                flipped = flip_psum.tile([P, len(step) * P], F32, name="flipped")
                for q, k in enumerate(step):
                    nc.tensor.transpose(
                        flipped[:, q * P : (q + 1) * P], tokens[b][:, k * P : (k + 1) * P], identity[:]
                    )
                nc.scalar.activation(tokens_t[:, step[0] * P : (step[-1] + 1) * P], flipped[:], COPY)

            acc = [
                acc_psum.tile([P, cols.stop - cols.start], F32, name=f"acc{h}") for h, cols in enumerate(PIECES)
            ]

            def multiply(k, h):
                nc.tensor.matmul(
                    acc[h][:],
                    tokens_t[:, k * P : (k + 1) * P],
                    weight_bf[k][:, PIECES[h]],
                    start=(k == 0),
                    stop=(k == K_TILES - 1),
                )

            last_steps = 1 if b == 0 else 2
            for i, step in enumerate(STEPS):
                flip(step)
                if 0 < i <= len(STEPS) - last_steps:
                    for h in range(len(PIECES)):
                        for k in STEPS[i - 1]:
                            multiply(k, h)
            for h in range(len(PIECES)):
                for step in STEPS[-last_steps:]:
                    for k in step:
                        multiply(k, h)

            rotated = held.tile([P, HIDDEN], F32, name=f"rotated{b}")
            for h, cols in enumerate(PIECES):
                if b == 0 and h == 0:
                    nc.vector.tensor_copy(rotated[:, cols], acc[h][:])
                else:
                    nc.scalar.activation(rotated[:, cols], acc[h][:], COPY)

            nc.vector.tensor_tensor(windows[b][:].indirect(offsets[:]), rotated[:], tokens[b][:], ADD)
            nc.sync.dma_start(out[b * P : (b + 1) * P, :], windows[b][:])
